import numpy as np
import ml_dtypes

BF16 = ml_dtypes.bfloat16


def bf(x):
    return np.asarray(x, np.float32).astype(BF16)


def f32(x):
    return np.asarray(x, np.float32)


def f64(x):
    return np.asarray(x).astype(np.float64)


def striped(idx):
    return np.tile(idx.reshape(-1, 16).T, (8, 1))


C, S, N = 256, 2048, 1024


def silu(v):
    return v / (1.0 + np.exp(-v))


def setup_inputs():
    return {
        "tok_emb": f32(np.random.standard_normal((C, S))),
        "pos_emb": f32(np.random.standard_normal((C, N))),
        "w1": bf(np.random.standard_normal((C, C)) / np.sqrt(C)),
        "b1": f32(0.2 * np.random.standard_normal((C, 1))),
        "w2": bf(np.random.standard_normal((C, C)) / np.sqrt(C)),
        "b2": f32(0.2 * np.random.standard_normal((C, 1))),
        "offs": striped(np.random.permutation(np.tile(np.arange(S), 2))[:N]),
    }


def reference(tok_emb, pos_emb, w1, b1, w2, b2, offs):
    idx = offs[:16].T.reshape(-1)
    h = f64(tok_emb)[:, idx] + f64(pos_emb)
    u = silu(f64(w1).T @ h + f64(b1))
    p = f64(w2).T @ u + f64(b2)
    return np.concatenate([h, p], axis=0)

@@ -1,0 +1,72 @@
+import concourse.mybir as mybir
+
+F32, BF16, U16 = mybir.dt.float32, mybir.dt.bfloat16, mybir.dt.uint16
+ADD = mybir.AluOpType.add
+SILU = mybir.ActivationFunctionType.Silu
+
+P = 128
+C = 256
+BLOCKS = C // P
+WORDS = 2048
+N = 1024
+BANK = 512
+HALVES = N // BANK
+
+FLOPS = 2 * 2 * C * C * N
+
+
+def tile_kanex_kernel(tc, tok_emb, pos_emb, w1, b1, w2, b2, offs, out):
+    nc = tc.nc
+    with (
+        tc.tile_pool(name="held", bufs=1) as held,
+        tc.psum_pool(name="psum", bufs=2) as psum,
+    ):
+        offsets = held.tile([P, N // 16], U16, name="offsets")
+        nc.sync.dma_start(offsets[:], offs)
+
+        table = [held.tile([P, WORDS], F32, name=f"table{b}") for b in range(BLOCKS)]
+        pos = [held.tile([P, N], F32, name=f"pos{b}") for b in range(BLOCKS)]
+        for b in range(BLOCKS):
+            rows = slice(b * P, (b + 1) * P)
+            nc.sync.dma_start(table[b][:], tok_emb[rows, :])
+            nc.sync.dma_start(pos[b][:], pos_emb[rows, :])
+
+        w1_sb = [held.tile([P, C], BF16, name=f"w1_sb{b}") for b in range(BLOCKS)]
+        w2_sb = [held.tile([P, C], BF16, name=f"w2_sb{b}") for b in range(BLOCKS)]
+        b1_sb = [held.tile([P, 1], F32, name=f"b1_sb{b}") for b in range(BLOCKS)]
+        b2_sb = [held.tile([P, 1], F32, name=f"b2_sb{b}") for b in range(BLOCKS)]
+        for b in range(BLOCKS):
+            rows = slice(b * P, (b + 1) * P)
+            nc.scalar.dma_start(w1_sb[b][:], w1[rows, :])
+            nc.scalar.dma_start(b1_sb[b][:], b1[rows, :])
+            nc.scalar.dma_start(w2_sb[b][:], w2[rows, :])
+            nc.scalar.dma_start(b2_sb[b][:], b2[rows, :])
+
+        h = [held.tile([P, N], F32, name=f"h{b}") for b in range(BLOCKS)]
+        h_bf = [held.tile([P, N], BF16, name=f"h_bf{b}") for b in range(BLOCKS)]
+        for b in range(BLOCKS):
+            nc.vector.tensor_tensor(h[b][:], table[b][:].indirect(offsets[:]), pos[b][:], ADD)
+            nc.sync.dma_start(out[b * P : (b + 1) * P, :], h[b][:])
+            nc.vector.tensor_copy(h_bf[b][:], h[b][:])
+
+        u_bf = [held.tile([P, N], BF16, name=f"u_bf{m}") for m in range(BLOCKS)]
+        p_sb = [held.tile([P, N], F32, name=f"p_sb{m}") for m in range(BLOCKS)]
+        for half in range(HALVES):
+            cols = slice(half * BANK, (half + 1) * BANK)
+            for m in range(BLOCKS):
+                acc1 = psum.tile([P, BANK], F32, name="acc1")
+                for k in range(BLOCKS):
+                    nc.tensor.matmul(
+                        acc1[:], w1_sb[k][:, m * P : (m + 1) * P], h_bf[k][:, cols],
+                        start=(k == 0), stop=(k == BLOCKS - 1),
+                    )
+                nc.scalar.activation(u_bf[m][:, cols], acc1[:], SILU, bias=b1_sb[m][:])
+            for m in range(BLOCKS):
+                acc2 = psum.tile([P, BANK], F32, name="acc2")
+                for k in range(BLOCKS):
+                    nc.tensor.matmul(
+                        acc2[:], w2_sb[k][:, m * P : (m + 1) * P], u_bf[k][:, cols],
+                        start=(k == 0), stop=(k == BLOCKS - 1),
+                    )
+                nc.vector.tensor_scalar_add(p_sb[m][:, cols], acc2[:], b2_sb[m][:])
+                nc.sync.dma_start(out[C + m * P : C + (m + 1) * P, cols], p_sb[m][:, cols])

@@ -3,6 +3,7 @@ import concourse.mybir as mybir
 F32, BF16, U16 = mybir.dt.float32, mybir.dt.bfloat16, mybir.dt.uint16
 ADD = mybir.AluOpType.add
 SILU = mybir.ActivationFunctionType.Silu
+IDENTITY = mybir.ActivationFunctionType.Identity
 
 P = 128
 C = 256
@@ -17,56 +18,72 @@ FLOPS = 2 * 2 * C * C * N
 
 def tile_kanex_kernel(tc, tok_emb, pos_emb, w1, b1, w2, b2, offs, out):
     nc = tc.nc
+    halves = [slice(i * BANK, (i + 1) * BANK) for i in range(HALVES)]
+    blocks = [slice(b * P, (b + 1) * P) for b in range(BLOCKS)]
     with (
         tc.tile_pool(name="held", bufs=1) as held,
-        tc.psum_pool(name="psum", bufs=2) as psum,
+        tc.psum_pool(name="psum", bufs=1) as psum,
     ):
         offsets = held.tile([P, N // 16], U16, name="offsets")
         nc.sync.dma_start(offsets[:], offs)
 
         table = [held.tile([P, WORDS], F32, name=f"table{b}") for b in range(BLOCKS)]
         pos = [held.tile([P, N], F32, name=f"pos{b}") for b in range(BLOCKS)]
-        for b in range(BLOCKS):
-            rows = slice(b * P, (b + 1) * P)
-            nc.sync.dma_start(table[b][:], tok_emb[rows, :])
-            nc.sync.dma_start(pos[b][:], pos_emb[rows, :])
-
         w1_sb = [held.tile([P, C], BF16, name=f"w1_sb{b}") for b in range(BLOCKS)]
         w2_sb = [held.tile([P, C], BF16, name=f"w2_sb{b}") for b in range(BLOCKS)]
         b1_sb = [held.tile([P, 1], F32, name=f"b1_sb{b}") for b in range(BLOCKS)]
         b2_sb = [held.tile([P, 1], F32, name=f"b2_sb{b}") for b in range(BLOCKS)]
+
+        nc.sync.dma_start(table[0][:], tok_emb[blocks[0], :])
+        nc.sync.dma_start(pos[0][:], pos_emb[blocks[0], :])
+        nc.sync.dma_start(table[1][:], tok_emb[blocks[1], :])
+        nc.sync.dma_start(pos[1][:, halves[0]], pos_emb[blocks[1], halves[0]])
         for b in range(BLOCKS):
-            rows = slice(b * P, (b + 1) * P)
-            nc.scalar.dma_start(w1_sb[b][:], w1[rows, :])
-            nc.scalar.dma_start(b1_sb[b][:], b1[rows, :])
-            nc.scalar.dma_start(w2_sb[b][:], w2[rows, :])
-            nc.scalar.dma_start(b2_sb[b][:], b2[rows, :])
+            nc.sync.dma_start(w1_sb[b][:], w1[blocks[b], :])
+        nc.sync.dma_start(pos[1][:, halves[1]], pos_emb[blocks[1], halves[1]])
+        for b in range(BLOCKS):
+            nc.sync.dma_start(w2_sb[b][:], w2[blocks[b], :])
+        for b in range(BLOCKS):
+            nc.scalar.dma_start(b1_sb[b][:], b1[blocks[b], :])
+            nc.scalar.dma_start(b2_sb[b][:], b2[blocks[b], :])
 
         h = [held.tile([P, N], F32, name=f"h{b}") for b in range(BLOCKS)]
         h_bf = [held.tile([P, N], BF16, name=f"h_bf{b}") for b in range(BLOCKS)]
-        for b in range(BLOCKS):
-            nc.vector.tensor_tensor(h[b][:], table[b][:].indirect(offsets[:]), pos[b][:], ADD)
-            nc.sync.dma_start(out[b * P : (b + 1) * P, :], h[b][:])
-            nc.vector.tensor_copy(h_bf[b][:], h[b][:])
-
         u_bf = [held.tile([P, N], BF16, name=f"u_bf{m}") for m in range(BLOCKS)]
         p_sb = [held.tile([P, N], F32, name=f"p_sb{m}") for m in range(BLOCKS)]
-        for half in range(HALVES):
-            cols = slice(half * BANK, (half + 1) * BANK)
+        acc1 = [[psum.tile([P, BANK], F32, name=f"acc1_{m}_{i}") for i in range(HALVES)] for m in range(BLOCKS)]
+        acc2 = [[psum.tile([P, BANK], F32, name=f"acc2_{m}_{i}") for i in range(HALVES)] for m in range(BLOCKS)]
+
+        def lookup_add(b, i):
+            piece = offsets[:, i * (BANK // 16) : (i + 1) * (BANK // 16)]
+            nc.vector.tensor_tensor(h[b][:, halves[i]], table[b][:].indirect(piece), pos[b][:, halves[i]], ADD)
+            nc.sync.dma_start(out[blocks[b], halves[i]], h[b][:, halves[i]])
+
+        def layer1(k, i):
             for m in range(BLOCKS):
-                acc1 = psum.tile([P, BANK], F32, name="acc1")
-                for k in range(BLOCKS):
+                nc.tensor.matmul(
+                    acc1[m][i][:], w1_sb[k][:, blocks[m]], h_bf[k][:, halves[i]],
+                    start=(k == 0), stop=(k == BLOCKS - 1),
+                )
+
+        for i in range(HALVES):
+            lookup_add(0, i)
+            nc.scalar.copy(h_bf[0][:, halves[i]], h[0][:, halves[i]])
+            layer1(0, i)
+
+        for i in range(HALVES):
+            lookup_add(1, i)
+            nc.vector.tensor_copy(h_bf[1][:, halves[i]], h[1][:, halves[i]])
+            layer1(1, i)
+            for m in range(BLOCKS):
+                nc.scalar.activation(u_bf[m][:, halves[i]], acc1[m][i][:], SILU, bias=b1_sb[m][:])
+            for k in range(BLOCKS):
+                for m in range(BLOCKS):
                     nc.tensor.matmul(
-                        acc1[:], w1_sb[k][:, m * P : (m + 1) * P], h_bf[k][:, cols],
+                        acc2[m][i][:], w2_sb[k][:, blocks[m]], u_bf[k][:, halves[i]],
                         start=(k == 0), stop=(k == BLOCKS - 1),
                     )
-                nc.scalar.activation(u_bf[m][:, cols], acc1[:], SILU, bias=b1_sb[m][:])
-            for m in range(BLOCKS):
-                acc2 = psum.tile([P, BANK], F32, name="acc2")
-                for k in range(BLOCKS):
-                    nc.tensor.matmul(
-                        acc2[:], w2_sb[k][:, m * P : (m + 1) * P], u_bf[k][:, cols],
-                        start=(k == 0), stop=(k == BLOCKS - 1),
-                    )
-                nc.vector.tensor_scalar_add(p_sb[m][:, cols], acc2[:], b2_sb[m][:])
-                nc.sync.dma_start(out[C + m * P : C + (m + 1) * P, cols], p_sb[m][:, cols])
+            nc.vector.tensor_scalar_add(p_sb[0][:, halves[i]], acc2[0][i][:], b2_sb[0][:])
+            nc.sync.dma_start(out[C : C + P, halves[i]], p_sb[0][:, halves[i]])
+            nc.scalar.activation(p_sb[1][:, halves[i]], acc2[1][i][:], IDENTITY, bias=b2_sb[1][:])
+            nc.scalar.dma_start(out[C + P : C + 2 * P, halves[i]], p_sb[1][:, halves[i]])

@@ -10,80 +10,84 @@ C = 256
 BLOCKS = C // P
 WORDS = 2048
 N = 1024
-BANK = 512
-HALVES = N // BANK
+PIECE = 256
+PIECES = N // PIECE
+BANKS = 8
 
 FLOPS = 2 * 2 * C * C * N
 
 
 def tile_kanex_kernel(tc, tok_emb, pos_emb, w1, b1, w2, b2, offs, out):
     nc = tc.nc
-    halves = [slice(i * BANK, (i + 1) * BANK) for i in range(HALVES)]
     blocks = [slice(b * P, (b + 1) * P) for b in range(BLOCKS)]
+    pieces = [slice(j * PIECE, (j + 1) * PIECE) for j in range(PIECES)]
     with (
         tc.tile_pool(name="held", bufs=1) as held,
-        tc.psum_pool(name="psum", bufs=1) as psum,
+        tc.psum_pool(name="psum", bufs=BANKS) as psum,
     ):
         offsets = held.tile([P, N // 16], U16, name="offsets")
         nc.sync.dma_start(offsets[:], offs)
 
         table = [held.tile([P, WORDS], F32, name=f"table{b}") for b in range(BLOCKS)]
         pos = [held.tile([P, N], F32, name=f"pos{b}") for b in range(BLOCKS)]
-        w1_sb = [held.tile([P, C], BF16, name=f"w1_sb{b}") for b in range(BLOCKS)]
-        w2_sb = [held.tile([P, C], BF16, name=f"w2_sb{b}") for b in range(BLOCKS)]
-        b1_sb = [held.tile([P, 1], F32, name=f"b1_sb{b}") for b in range(BLOCKS)]
-        b2_sb = [held.tile([P, 1], F32, name=f"b2_sb{b}") for b in range(BLOCKS)]
+        w1_sb = held.tile([P, BLOCKS, C], BF16, name="w1_sb")
+        w2_sb = held.tile([P, BLOCKS, C], BF16, name="w2_sb")
+        b1_sb = [held.tile([P, 1], F32, name=f"b1_sb{m}") for m in range(BLOCKS)]
+        b2_sb = [held.tile([P, 1], F32, name=f"b2_sb{m}") for m in range(BLOCKS)]
 
         nc.sync.dma_start(table[0][:], tok_emb[blocks[0], :])
         nc.sync.dma_start(pos[0][:], pos_emb[blocks[0], :])
+        nc.sync.dma_start(w1_sb[:], w1.rearrange("(k p) m -> p k m", p=P))
         nc.sync.dma_start(table[1][:], tok_emb[blocks[1], :])
-        nc.sync.dma_start(pos[1][:, halves[0]], pos_emb[blocks[1], halves[0]])
-        for b in range(BLOCKS):
-            nc.sync.dma_start(w1_sb[b][:], w1[blocks[b], :])
-        nc.sync.dma_start(pos[1][:, halves[1]], pos_emb[blocks[1], halves[1]])
-        for b in range(BLOCKS):
-            nc.sync.dma_start(w2_sb[b][:], w2[blocks[b], :])
-        for b in range(BLOCKS):
-            nc.scalar.dma_start(b1_sb[b][:], b1[blocks[b], :])
-            nc.scalar.dma_start(b2_sb[b][:], b2[blocks[b], :])
+        nc.sync.dma_start(pos[1][:, : N // 2], pos_emb[blocks[1], : N // 2])
+        nc.sync.dma_start(pos[1][:, N // 2 :], pos_emb[blocks[1], N // 2 :])
+        nc.sync.dma_start(w2_sb[:], w2.rearrange("(k p) m -> p k m", p=P))
+        for m in range(BLOCKS):
+            nc.scalar.dma_start(b1_sb[m][:], b1[blocks[m], :])
+            nc.scalar.dma_start(b2_sb[m][:], b2[blocks[m], :])
 
         h = [held.tile([P, N], F32, name=f"h{b}") for b in range(BLOCKS)]
         h_bf = [held.tile([P, N], BF16, name=f"h_bf{b}") for b in range(BLOCKS)]
         u_bf = [held.tile([P, N], BF16, name=f"u_bf{m}") for m in range(BLOCKS)]
-        p_sb = [held.tile([P, N], F32, name=f"p_sb{m}") for m in range(BLOCKS)]
-        acc1 = [[psum.tile([P, BANK], F32, name=f"acc1_{m}_{i}") for i in range(HALVES)] for m in range(BLOCKS)]
-        acc2 = [[psum.tile([P, BANK], F32, name=f"acc2_{m}_{i}") for i in range(HALVES)] for m in range(BLOCKS)]
+        p_sb = held.tile([P, BLOCKS, N], F32, name="p_sb")
 
-        def lookup_add(b, i):
-            piece = offsets[:, i * (BANK // 16) : (i + 1) * (BANK // 16)]
-            nc.vector.tensor_tensor(h[b][:, halves[i]], table[b][:].indirect(piece), pos[b][:, halves[i]], ADD)
-            nc.sync.dma_start(out[blocks[b], halves[i]], h[b][:, halves[i]])
+        def lookup_add(b, j):
+            some = offsets[:, j * (PIECE // 16) : (j + 1) * (PIECE // 16)]
+            nc.vector.tensor_tensor(h[b][:, pieces[j]], table[b][:].indirect(some), pos[b][:, pieces[j]], ADD)
 
-        def layer1(k, i):
+        def layer1(k, j):
             for m in range(BLOCKS):
                 nc.tensor.matmul(
-                    acc1[m][i][:], w1_sb[k][:, blocks[m]], h_bf[k][:, halves[i]],
+                    acc1[j][m][:], w1_sb[:, k, blocks[m]], h_bf[k][:, pieces[j]],
                     start=(k == 0), stop=(k == BLOCKS - 1),
                 )
 
-        for i in range(HALVES):
-            lookup_add(0, i)
-            nc.scalar.copy(h_bf[0][:, halves[i]], h[0][:, halves[i]])
-            layer1(0, i)
-
-        for i in range(HALVES):
-            lookup_add(1, i)
-            nc.vector.tensor_copy(h_bf[1][:, halves[i]], h[1][:, halves[i]])
-            layer1(1, i)
-            for m in range(BLOCKS):
-                nc.scalar.activation(u_bf[m][:, halves[i]], acc1[m][i][:], SILU, bias=b1_sb[m][:])
+        def layer2(j):
+            acc2 = [psum.tile([P, PIECE], F32, name="acc") for m in range(BLOCKS)]
             for k in range(BLOCKS):
                 for m in range(BLOCKS):
                     nc.tensor.matmul(
-                        acc2[m][i][:], w2_sb[k][:, blocks[m]], u_bf[k][:, halves[i]],
+                        acc2[m][:], w2_sb[:, k, blocks[m]], u_bf[k][:, pieces[j]],
                         start=(k == 0), stop=(k == BLOCKS - 1),
                     )
-            nc.vector.tensor_scalar_add(p_sb[0][:, halves[i]], acc2[0][i][:], b2_sb[0][:])
-            nc.sync.dma_start(out[C : C + P, halves[i]], p_sb[0][:, halves[i]])
-            nc.scalar.activation(p_sb[1][:, halves[i]], acc2[1][i][:], IDENTITY, bias=b2_sb[1][:])
-            nc.scalar.dma_start(out[C + P : C + 2 * P, halves[i]], p_sb[1][:, halves[i]])
+            nc.vector.tensor_scalar_add(p_sb[:, 0, pieces[j]], acc2[0][:], b2_sb[0][:])
+            nc.scalar.activation(p_sb[:, 1, pieces[j]], acc2[1][:], IDENTITY, bias=b2_sb[1][:])
+            nc.sync.dma_start(out[C:, pieces[j]].rearrange("(m p) n -> p m n", p=P), p_sb[:, :, pieces[j]])
+
+        acc1 = [[psum.tile([P, PIECE], F32, name="acc") for m in range(BLOCKS)] for j in range(PIECES)]
+        for j in range(PIECES):
+            lookup_add(0, j)
+            nc.scalar.copy(h_bf[0][:, pieces[j]], h[0][:, pieces[j]])
+            layer1(0, j)
+        nc.sync.dma_start(out[blocks[0], :], h[0][:])
+
+        for j in range(PIECES):
+            lookup_add(1, j)
+            nc.vector.tensor_copy(h_bf[1][:, pieces[j]], h[1][:, pieces[j]])
+            layer1(1, j)
+            for m in range(BLOCKS):
+                nc.scalar.activation(u_bf[m][:, pieces[j]], acc1[j][m][:], SILU, bias=b1_sb[m][:])
+            if j > 0:
+                layer2(j - 1)
+        nc.sync.dma_start(out[blocks[1], :], h[1][:])
+        layer2(PIECES - 1)

@@ -71,7 +71,10 @@ def tile_kanex_kernel(tc, tok_emb, pos_emb, w1, b1, w2, b2, offs, out):
                         start=(k == 0), stop=(k == BLOCKS - 1),
                     )
             nc.vector.tensor_scalar_add(p_sb[:, 0, pieces[j]], acc2[0][:], b2_sb[0][:])
-            nc.scalar.activation(p_sb[:, 1, pieces[j]], acc2[1][:], IDENTITY, bias=b2_sb[1][:])
+            if j < PIECES - 1:
+                nc.vector.tensor_scalar_add(p_sb[:, 1, pieces[j]], acc2[1][:], b2_sb[1][:])
+            else:
+                nc.scalar.activation(p_sb[:, 1, pieces[j]], acc2[1][:], IDENTITY, bias=b2_sb[1][:])
             nc.sync.dma_start(out[C:, pieces[j]].rearrange("(m p) n -> p m n", p=P), p_sb[:, :, pieces[j]])
 
         acc1 = [[psum.tile([P, PIECE], F32, name="acc") for m in range(BLOCKS)] for j in range(PIECES)]
@@ -83,7 +86,7 @@ def tile_kanex_kernel(tc, tok_emb, pos_emb, w1, b1, w2, b2, offs, out):
 
         for j in range(PIECES):
             lookup_add(1, j)
-            nc.vector.tensor_copy(h_bf[1][:, pieces[j]], h[1][:, pieces[j]])
+            nc.gpsimd.tensor_copy(h_bf[1][:, pieces[j]], h[1][:, pieces[j]])
             layer1(1, j)
             for m in range(BLOCKS):
                 nc.scalar.activation(u_bf[m][:, pieces[j]], acc1[j][m][:], SILU, bias=b1_sb[m][:])

@@ -41,10 +41,11 @@ def tile_kanex_kernel(tc, tok_emb, pos_emb, w1, b1, w2, b2, offs, out):
         nc.sync.dma_start(table[1][:], tok_emb[blocks[1], :])
         nc.sync.dma_start(pos[1][:, : N // 2], pos_emb[blocks[1], : N // 2])
         nc.sync.dma_start(pos[1][:, N // 2 :], pos_emb[blocks[1], N // 2 :])
+        for m in range(BLOCKS):
+            nc.sync.dma_start(b1_sb[m][:], b1[blocks[m], :])
         nc.sync.dma_start(w2_sb[:], w2.rearrange("(k p) m -> p k m", p=P))
         for m in range(BLOCKS):
-            nc.scalar.dma_start(b1_sb[m][:], b1[blocks[m], :])
-            nc.scalar.dma_start(b2_sb[m][:], b2[blocks[m], :])
+            nc.sync.dma_start(b2_sb[m][:], b2[blocks[m], :])
 
         h = [held.tile([P, N], F32, name=f"h{b}") for b in range(BLOCKS)]
         h_bf = [held.tile([P, N], BF16, name=f"h_bf{b}") for b in range(BLOCKS)]
@@ -71,10 +72,7 @@ def tile_kanex_kernel(tc, tok_emb, pos_emb, w1, b1, w2, b2, offs, out):
                         start=(k == 0), stop=(k == BLOCKS - 1),
                     )
             nc.vector.tensor_scalar_add(p_sb[:, 0, pieces[j]], acc2[0][:], b2_sb[0][:])
-            if j < PIECES - 1:
-                nc.vector.tensor_scalar_add(p_sb[:, 1, pieces[j]], acc2[1][:], b2_sb[1][:])
-            else:
-                nc.scalar.activation(p_sb[:, 1, pieces[j]], acc2[1][:], IDENTITY, bias=b2_sb[1][:])
+            nc.scalar.activation(p_sb[:, 1, pieces[j]], acc2[1][:], IDENTITY, bias=b2_sb[1][:])
             nc.sync.dma_start(out[C:, pieces[j]].rearrange("(m p) n -> p m n", p=P), p_sb[:, :, pieces[j]])
 
         acc1 = [[psum.tile([P, PIECE], F32, name="acc") for m in range(BLOCKS)] for j in range(PIECES)]
@@ -86,7 +84,7 @@ def tile_kanex_kernel(tc, tok_emb, pos_emb, w1, b1, w2, b2, offs, out):
 
         for j in range(PIECES):
             lookup_add(1, j)
-            nc.gpsimd.tensor_copy(h_bf[1][:, pieces[j]], h[1][:, pieces[j]])
+            nc.vector.tensor_copy(h_bf[1][:, pieces[j]], h[1][:, pieces[j]])
             layer1(1, j)
             for m in range(BLOCKS):
                 nc.scalar.activation(u_bf[m][:, pieces[j]], acc1[j][m][:], SILU, bias=b1_sb[m][:])

@@ -41,11 +41,10 @@ def tile_kanex_kernel(tc, tok_emb, pos_emb, w1, b1, w2, b2, offs, out):
         nc.sync.dma_start(table[1][:], tok_emb[blocks[1], :])
         nc.sync.dma_start(pos[1][:, : N // 2], pos_emb[blocks[1], : N // 2])
         nc.sync.dma_start(pos[1][:, N // 2 :], pos_emb[blocks[1], N // 2 :])
-        for m in range(BLOCKS):
-            nc.sync.dma_start(b1_sb[m][:], b1[blocks[m], :])
         nc.sync.dma_start(w2_sb[:], w2.rearrange("(k p) m -> p k m", p=P))
         for m in range(BLOCKS):
-            nc.sync.dma_start(b2_sb[m][:], b2[blocks[m], :])
+            nc.scalar.dma_start(b1_sb[m][:], b1[blocks[m], :])
+            nc.scalar.dma_start(b2_sb[m][:], b2[blocks[m], :])
 
         h = [held.tile([P, N], F32, name=f"h{b}") for b in range(BLOCKS)]
         h_bf = [held.tile([P, N], BF16, name=f"h_bf{b}") for b in range(BLOCKS)]
@@ -72,7 +71,10 @@ def tile_kanex_kernel(tc, tok_emb, pos_emb, w1, b1, w2, b2, offs, out):
                         start=(k == 0), stop=(k == BLOCKS - 1),
                     )
             nc.vector.tensor_scalar_add(p_sb[:, 0, pieces[j]], acc2[0][:], b2_sb[0][:])
-            nc.scalar.activation(p_sb[:, 1, pieces[j]], acc2[1][:], IDENTITY, bias=b2_sb[1][:])
+            if j < PIECES - 1:
+                nc.vector.tensor_scalar_add(p_sb[:, 1, pieces[j]], acc2[1][:], b2_sb[1][:])
+            else:
+                nc.scalar.activation(p_sb[:, 1, pieces[j]], acc2[1][:], IDENTITY, bias=b2_sb[1][:])
             nc.sync.dma_start(out[C:, pieces[j]].rearrange("(m p) n -> p m n", p=P), p_sb[:, :, pieces[j]])
 
         acc1 = [[psum.tile([P, PIECE], F32, name="acc") for m in range(BLOCKS)] for j in range(PIECES)]

@@ -54,6 +54,7 @@ def tile_kanex_kernel(tc, tok_emb, pos_emb, w1, b1, w2, b2, offs, out):
         def lookup_add(b, j):
             some = offsets[:, j * (PIECE // 16) : (j + 1) * (PIECE // 16)]
             nc.vector.tensor_tensor(h[b][:, pieces[j]], table[b][:].indirect(some), pos[b][:, pieces[j]], ADD)
+            nc.sync.dma_start(out[blocks[b], pieces[j]], h[b][:, pieces[j]])
 
         def layer1(k, j):
             for m in range(BLOCKS):
@@ -71,10 +72,7 @@ def tile_kanex_kernel(tc, tok_emb, pos_emb, w1, b1, w2, b2, offs, out):
                         start=(k == 0), stop=(k == BLOCKS - 1),
                     )
             nc.vector.tensor_scalar_add(p_sb[:, 0, pieces[j]], acc2[0][:], b2_sb[0][:])
-            if j < PIECES - 1:
-                nc.vector.tensor_scalar_add(p_sb[:, 1, pieces[j]], acc2[1][:], b2_sb[1][:])
-            else:
-                nc.scalar.activation(p_sb[:, 1, pieces[j]], acc2[1][:], IDENTITY, bias=b2_sb[1][:])
+            nc.scalar.activation(p_sb[:, 1, pieces[j]], acc2[1][:], IDENTITY, bias=b2_sb[1][:])
             nc.sync.dma_start(out[C:, pieces[j]].rearrange("(m p) n -> p m n", p=P), p_sb[:, :, pieces[j]])
 
         acc1 = [[psum.tile([P, PIECE], F32, name="acc") for m in range(BLOCKS)] for j in range(PIECES)]
@@ -82,7 +80,6 @@ def tile_kanex_kernel(tc, tok_emb, pos_emb, w1, b1, w2, b2, offs, out):
             lookup_add(0, j)
             nc.scalar.copy(h_bf[0][:, pieces[j]], h[0][:, pieces[j]])
             layer1(0, j)
-        nc.sync.dma_start(out[blocks[0], :], h[0][:])
 
         for j in range(PIECES):
             lookup_add(1, j)
@@ -92,5 +89,4 @@ def tile_kanex_kernel(tc, tok_emb, pos_emb, w1, b1, w2, b2, offs, out):
                 nc.scalar.activation(u_bf[m][:, pieces[j]], acc1[j][m][:], SILU, bias=b1_sb[m][:])
             if j > 0:
                 layer2(j - 1)
-        nc.sync.dma_start(out[blocks[1], :], h[1][:])
         layer2(PIECES - 1)

@@ -39,8 +39,8 @@ def tile_kanex_kernel(tc, tok_emb, pos_emb, w1, b1, w2, b2, offs, out):
         nc.sync.dma_start(pos[0][:], pos_emb[blocks[0], :])
         nc.sync.dma_start(w1_sb[:], w1.rearrange("(k p) m -> p k m", p=P))
         nc.sync.dma_start(table[1][:], tok_emb[blocks[1], :])
-        nc.sync.dma_start(pos[1][:, : N // 2], pos_emb[blocks[1], : N // 2])
-        nc.sync.dma_start(pos[1][:, N // 2 :], pos_emb[blocks[1], N // 2 :])
+        nc.sync.dma_start(pos[1][:, :PIECE], pos_emb[blocks[1], :PIECE])
+        nc.sync.dma_start(pos[1][:, PIECE:], pos_emb[blocks[1], PIECE:])
         nc.sync.dma_start(w2_sb[:], w2.rearrange("(k p) m -> p k m", p=P))
         for m in range(BLOCKS):
             nc.scalar.dma_start(b1_sb[m][:], b1[blocks[m], :])

@@ -10,9 +10,10 @@ C = 256
 BLOCKS = C // P
 WORDS = 2048
 N = 1024
-PIECE = 256
-PIECES = N // PIECE
+WIDTHS = (256, 256, 256, 256)
+PIECES = len(WIDTHS)
 BANKS = 8
+PER_COLUMN = 16
 
 FLOPS = 2 * 2 * C * C * N
 
@@ -20,12 +21,12 @@ FLOPS = 2 * 2 * C * C * N
 def tile_kanex_kernel(tc, tok_emb, pos_emb, w1, b1, w2, b2, offs, out):
     nc = tc.nc
     blocks = [slice(b * P, (b + 1) * P) for b in range(BLOCKS)]
-    pieces = [slice(j * PIECE, (j + 1) * PIECE) for j in range(PIECES)]
+    pieces = [slice(sum(WIDTHS[:j]), sum(WIDTHS[: j + 1])) for j in range(PIECES)]
     with (
         tc.tile_pool(name="held", bufs=1) as held,
         tc.psum_pool(name="psum", bufs=BANKS) as psum,
     ):
-        offsets = held.tile([P, N // 16], U16, name="offsets")
+        offsets = held.tile([P, N // PER_COLUMN], U16, name="offsets")
         nc.sync.dma_start(offsets[:], offs)
 
         table = [held.tile([P, WORDS], F32, name=f"table{b}") for b in range(BLOCKS)]
@@ -35,12 +36,17 @@ def tile_kanex_kernel(tc, tok_emb, pos_emb, w1, b1, w2, b2, offs, out):
         b1_sb = [held.tile([P, 1], F32, name=f"b1_sb{m}") for m in range(BLOCKS)]
         b2_sb = [held.tile([P, 1], F32, name=f"b2_sb{m}") for m in range(BLOCKS)]
 
+        zeros = held.tile([P, 1], F32, name="zeros")
+        unread = held.tile([P, 1], F32, name="unread")
+        nc.vector.memset(zeros[:], 0.0)
+        nc.scalar.activation(unread[:], zeros[:], SILU)
+
         nc.sync.dma_start(table[0][:], tok_emb[blocks[0], :])
         nc.sync.dma_start(pos[0][:], pos_emb[blocks[0], :])
         nc.sync.dma_start(w1_sb[:], w1.rearrange("(k p) m -> p k m", p=P))
         nc.sync.dma_start(table[1][:], tok_emb[blocks[1], :])
-        nc.sync.dma_start(pos[1][:, :PIECE], pos_emb[blocks[1], :PIECE])
-        nc.sync.dma_start(pos[1][:, PIECE:], pos_emb[blocks[1], PIECE:])
+        nc.sync.dma_start(pos[1][:, : WIDTHS[0]], pos_emb[blocks[1], : WIDTHS[0]])
+        nc.sync.dma_start(pos[1][:, WIDTHS[0] :], pos_emb[blocks[1], WIDTHS[0] :])
         nc.sync.dma_start(w2_sb[:], w2.rearrange("(k p) m -> p k m", p=P))
         for m in range(BLOCKS):
             nc.scalar.dma_start(b1_sb[m][:], b1[blocks[m], :])
@@ -52,7 +58,7 @@ def tile_kanex_kernel(tc, tok_emb, pos_emb, w1, b1, w2, b2, offs, out):
         p_sb = held.tile([P, BLOCKS, N], F32, name="p_sb")
 
         def lookup_add(b, j):
-            some = offsets[:, j * (PIECE // 16) : (j + 1) * (PIECE // 16)]
+            some = offsets[:, pieces[j].start // PER_COLUMN : pieces[j].stop // PER_COLUMN]
             nc.vector.tensor_tensor(h[b][:, pieces[j]], table[b][:].indirect(some), pos[b][:, pieces[j]], ADD)
             nc.sync.dma_start(out[blocks[b], pieces[j]], h[b][:, pieces[j]])
 
@@ -64,7 +70,7 @@ def tile_kanex_kernel(tc, tok_emb, pos_emb, w1, b1, w2, b2, offs, out):
                 )
 
         def layer2(j):
-            acc2 = [psum.tile([P, PIECE], F32, name="acc") for m in range(BLOCKS)]
+            acc2 = [psum.tile([P, WIDTHS[j]], F32, name="acc") for m in range(BLOCKS)]
             for k in range(BLOCKS):
                 for m in range(BLOCKS):
                     nc.tensor.matmul(
@@ -75,7 +81,7 @@ def tile_kanex_kernel(tc, tok_emb, pos_emb, w1, b1, w2, b2, offs, out):
             nc.scalar.activation(p_sb[:, 1, pieces[j]], acc2[1][:], IDENTITY, bias=b2_sb[1][:])
             nc.sync.dma_start(out[C:, pieces[j]].rearrange("(m p) n -> p m n", p=P), p_sb[:, :, pieces[j]])
 
-        acc1 = [[psum.tile([P, PIECE], F32, name="acc") for m in range(BLOCKS)] for j in range(PIECES)]
+        acc1 = [[psum.tile([P, WIDTHS[j]], F32, name="acc") for m in range(BLOCKS)] for j in range(PIECES)]
         for j in range(PIECES):
             lookup_add(0, j)
             nc.scalar.copy(h_bf[0][:, pieces[j]], h[0][:, pieces[j]])

@@ -20,7 +20,10 @@ FLOPS = 2 * 2 * C * C * N
 
 def tile_kanex_kernel(tc, tok_emb, pos_emb, w1, b1, w2, b2, offs, out):
     nc = tc.nc
-    blocks = [slice(b * P, (b + 1) * P) for b in range(BLOCKS)]
+    tok_blocks = tok_emb.rearrange("(p b) s -> p b s", b=BLOCKS)
+    pos_blocks = pos_emb.rearrange("(p b) n -> p b n", b=BLOCKS)
+    h_out = out[:C, :].rearrange("(p b) n -> p b n", b=BLOCKS)
+    p_out = out[C:, :].rearrange("(p b) n -> p b n", b=BLOCKS)
     pieces = [slice(sum(WIDTHS[:j]), sum(WIDTHS[: j + 1])) for j in range(PIECES)]
     with (
         tc.tile_pool(name="held", bufs=1) as held,
@@ -33,24 +36,23 @@ def tile_kanex_kernel(tc, tok_emb, pos_emb, w1, b1, w2, b2, offs, out):
         pos = [held.tile([P, N], F32, name=f"pos{b}") for b in range(BLOCKS)]
         w1_sb = held.tile([P, BLOCKS, C], BF16, name="w1_sb")
         w2_sb = held.tile([P, BLOCKS, C], BF16, name="w2_sb")
-        b1_sb = [held.tile([P, 1], F32, name=f"b1_sb{m}") for m in range(BLOCKS)]
-        b2_sb = [held.tile([P, 1], F32, name=f"b2_sb{m}") for m in range(BLOCKS)]
+        b1_sb = held.tile([P, BLOCKS], F32, name="b1_sb")
+        b2_sb = held.tile([P, BLOCKS], F32, name="b2_sb")
 
         zeros = held.tile([P, 1], F32, name="zeros")
         unread = held.tile([P, 1], F32, name="unread")
         nc.vector.memset(zeros[:], 0.0)
         nc.scalar.activation(unread[:], zeros[:], SILU)
 
-        nc.sync.dma_start(table[0][:], tok_emb[blocks[0], :])
-        nc.sync.dma_start(pos[0][:], pos_emb[blocks[0], :])
-        nc.sync.dma_start(w1_sb[:], w1.rearrange("(k p) m -> p k m", p=P))
-        nc.sync.dma_start(table[1][:], tok_emb[blocks[1], :])
-        nc.sync.dma_start(pos[1][:, : WIDTHS[0]], pos_emb[blocks[1], : WIDTHS[0]])
-        nc.sync.dma_start(pos[1][:, WIDTHS[0] :], pos_emb[blocks[1], WIDTHS[0] :])
-        nc.sync.dma_start(w2_sb[:], w2.rearrange("(k p) m -> p k m", p=P))
-        for m in range(BLOCKS):
-            nc.scalar.dma_start(b1_sb[m][:], b1[blocks[m], :])
-            nc.scalar.dma_start(b2_sb[m][:], b2[blocks[m], :])
+        nc.sync.dma_start(table[0][:], tok_blocks[:, 0, :])
+        nc.sync.dma_start(pos[0][:], pos_blocks[:, 0, :])
+        nc.sync.dma_start(w1_sb[:], w1.rearrange("(p k) m -> p k m", k=BLOCKS))
+        nc.sync.dma_start(table[1][:], tok_blocks[:, 1, :])
+        nc.sync.dma_start(pos[1][:, : WIDTHS[0]], pos_blocks[:, 1, : WIDTHS[0]])
+        nc.sync.dma_start(pos[1][:, WIDTHS[0] :], pos_blocks[:, 1, WIDTHS[0] :])
+        nc.sync.dma_start(w2_sb[:], w2.rearrange("(p k) m -> p k m", k=BLOCKS))
+        nc.scalar.dma_start(b1_sb[:], b1.rearrange("(p m) o -> p (m o)", m=BLOCKS))
+        nc.scalar.dma_start(b2_sb[:], b2.rearrange("(p m) o -> p (m o)", m=BLOCKS))
 
         h = [held.tile([P, N], F32, name=f"h{b}") for b in range(BLOCKS)]
         h_bf = [held.tile([P, N], BF16, name=f"h_bf{b}") for b in range(BLOCKS)]
@@ -60,12 +62,12 @@ def tile_kanex_kernel(tc, tok_emb, pos_emb, w1, b1, w2, b2, offs, out):
         def lookup_add(b, j):
             some = offsets[:, pieces[j].start // PER_COLUMN : pieces[j].stop // PER_COLUMN]
             nc.vector.tensor_tensor(h[b][:, pieces[j]], table[b][:].indirect(some), pos[b][:, pieces[j]], ADD)
-            nc.sync.dma_start(out[blocks[b], pieces[j]], h[b][:, pieces[j]])
+            nc.sync.dma_start(h_out[:, b, pieces[j]], h[b][:, pieces[j]])
 
         def layer1(k, j):
             for m in range(BLOCKS):
                 nc.tensor.matmul(
-                    acc1[j][m][:], w1_sb[:, k, blocks[m]], h_bf[k][:, pieces[j]],
+                    acc1[j][m][:], w1_sb[:, k, m::BLOCKS], h_bf[k][:, pieces[j]],
                     start=(k == 0), stop=(k == BLOCKS - 1),
                 )
 
@@ -74,12 +76,12 @@ def tile_kanex_kernel(tc, tok_emb, pos_emb, w1, b1, w2, b2, offs, out):
             for k in range(BLOCKS):
                 for m in range(BLOCKS):
                     nc.tensor.matmul(
-                        acc2[m][:], w2_sb[:, k, blocks[m]], u_bf[k][:, pieces[j]],
+                        acc2[m][:], w2_sb[:, k, m::BLOCKS], u_bf[k][:, pieces[j]],
                         start=(k == 0), stop=(k == BLOCKS - 1),
                     )
-            nc.vector.tensor_scalar_add(p_sb[:, 0, pieces[j]], acc2[0][:], b2_sb[0][:])
-            nc.scalar.activation(p_sb[:, 1, pieces[j]], acc2[1][:], IDENTITY, bias=b2_sb[1][:])
-            nc.sync.dma_start(out[C:, pieces[j]].rearrange("(m p) n -> p m n", p=P), p_sb[:, :, pieces[j]])
+            nc.vector.tensor_scalar_add(p_sb[:, 0, pieces[j]], acc2[0][:], b2_sb[:, 0:1])
+            nc.scalar.activation(p_sb[:, 1, pieces[j]], acc2[1][:], IDENTITY, bias=b2_sb[:, 1:2])
+            nc.sync.dma_start(p_out[:, :, pieces[j]], p_sb[:, :, pieces[j]])
 
         acc1 = [[psum.tile([P, WIDTHS[j]], F32, name="acc") for m in range(BLOCKS)] for j in range(PIECES)]
         for j in range(PIECES):
@@ -92,7 +94,7 @@ def tile_kanex_kernel(tc, tok_emb, pos_emb, w1, b1, w2, b2, offs, out):
             nc.vector.tensor_copy(h_bf[1][:, pieces[j]], h[1][:, pieces[j]])
             layer1(1, j)
             for m in range(BLOCKS):
-                nc.scalar.activation(u_bf[m][:, pieces[j]], acc1[j][m][:], SILU, bias=b1_sb[m][:])
+                nc.scalar.activation(u_bf[m][:, pieces[j]], acc1[j][m][:], SILU, bias=b1_sb[:, m : m + 1])
             if j > 0:
                 layer2(j - 1)
         layer2(PIECES - 1)

@@ -80,8 +80,17 @@ def tile_kanex_kernel(tc, tok_emb, pos_emb, w1, b1, w2, b2, offs, out):
                         start=(k == 0), stop=(k == BLOCKS - 1),
                     )
             nc.vector.tensor_scalar_add(p_sb[:, 0, pieces[j]], acc2[0][:], b2_sb[:, 0:1])
-            nc.scalar.activation(p_sb[:, 1, pieces[j]], acc2[1][:], IDENTITY, bias=b2_sb[:, 1:2])
-            nc.sync.dma_start(p_out[:, :, pieces[j]], p_sb[:, :, pieces[j]])
+            if j < PIECES // 2:
+                nc.vector.tensor_scalar_add(p_sb[:, 1, pieces[j]], acc2[1][:], b2_sb[:, 1:2])
+            else:
+                nc.scalar.activation(p_sb[:, 1, pieces[j]], acc2[1][:], IDENTITY, bias=b2_sb[:, 1:2])
+
+        def store_p(j):
+            if j < PIECES - 1:
+                nc.sync.dma_start(p_out[:, :, pieces[j]], p_sb[:, :, pieces[j]])
+            else:
+                for m in range(BLOCKS):
+                    nc.sync.dma_start(p_out[:, m, pieces[j]], p_sb[:, m, pieces[j]])
 
         acc1 = [[psum.tile([P, WIDTHS[j]], F32, name="acc") for m in range(BLOCKS)] for j in range(PIECES)]
         for j in range(PIECES):
@@ -95,6 +104,9 @@ def tile_kanex_kernel(tc, tok_emb, pos_emb, w1, b1, w2, b2, offs, out):
             layer1(1, j)
             for m in range(BLOCKS):
                 nc.scalar.activation(u_bf[m][:, pieces[j]], acc1[j][m][:], SILU, bias=b1_sb[:, m : m + 1])
-            if j > 0:
-                layer2(j - 1)
-        layer2(PIECES - 1)
+            if j == 1:
+                layer2(0)
+        store_p(0)
+        for j in range(1, PIECES):
+            layer2(j)
+            store_p(j)

@@ -62,7 +62,9 @@ def tile_kanex_kernel(tc, tok_emb, pos_emb, w1, b1, w2, b2, offs, out):
         def lookup_add(b, j):
             some = offsets[:, pieces[j].start // PER_COLUMN : pieces[j].stop // PER_COLUMN]
             nc.vector.tensor_tensor(h[b][:, pieces[j]], table[b][:].indirect(some), pos[b][:, pieces[j]], ADD)
-            nc.sync.dma_start(h_out[:, b, pieces[j]], h[b][:, pieces[j]])
+            if j % 2 == 1:
+                pair = slice(pieces[j - 1].start, pieces[j].stop)
+                nc.sync.dma_start(h_out[:, b, pair], h[b][:, pair])
 
         def layer1(k, j):
             for m in range(BLOCKS):
@@ -86,11 +88,8 @@ def tile_kanex_kernel(tc, tok_emb, pos_emb, w1, b1, w2, b2, offs, out):
                 nc.scalar.activation(p_sb[:, 1, pieces[j]], acc2[1][:], IDENTITY, bias=b2_sb[:, 1:2])
 
         def store_p(j):
-            if j < PIECES - 1:
-                nc.sync.dma_start(p_out[:, :, pieces[j]], p_sb[:, :, pieces[j]])
-            else:
-                for m in range(BLOCKS):
-                    nc.sync.dma_start(p_out[:, m, pieces[j]], p_sb[:, m, pieces[j]])
+            for m in range(BLOCKS):
+                nc.sync.dma_start(p_out[:, m, pieces[j]], p_sb[:, m, pieces[j]])
 
         acc1 = [[psum.tile([P, WIDTHS[j]], F32, name="acc") for m in range(BLOCKS)] for j in range(PIECES)]
         for j in range(PIECES):

@@ -30,7 +30,6 @@ def tile_kanex_kernel(tc, tok_emb, pos_emb, w1, b1, w2, b2, offs, out):
         tc.psum_pool(name="psum", bufs=BANKS) as psum,
     ):
         offsets = held.tile([P, N // PER_COLUMN], U16, name="offsets")
-        nc.sync.dma_start(offsets[:], offs)
 
         table = [held.tile([P, WORDS], F32, name=f"table{b}") for b in range(BLOCKS)]
         pos = [held.tile([P, N], F32, name=f"pos{b}") for b in range(BLOCKS)]
@@ -45,14 +44,15 @@ def tile_kanex_kernel(tc, tok_emb, pos_emb, w1, b1, w2, b2, offs, out):
         nc.scalar.activation(unread[:], zeros[:], SILU)
 
         nc.sync.dma_start(table[0][:], tok_blocks[:, 0, :])
+        nc.sync.dma_start(offsets[:], offs)
         nc.sync.dma_start(pos[0][:], pos_blocks[:, 0, :])
         nc.sync.dma_start(w1_sb[:], w1.rearrange("(p k) m -> p k m", k=BLOCKS))
         nc.sync.dma_start(table[1][:], tok_blocks[:, 1, :])
         nc.sync.dma_start(pos[1][:, : WIDTHS[0]], pos_blocks[:, 1, : WIDTHS[0]])
+        nc.sync.dma_start(b1_sb[:], b1.rearrange("(p m) o -> p (m o)", m=BLOCKS))
+        nc.sync.dma_start(b2_sb[:], b2.rearrange("(p m) o -> p (m o)", m=BLOCKS))
         nc.sync.dma_start(pos[1][:, WIDTHS[0] :], pos_blocks[:, 1, WIDTHS[0] :])
         nc.sync.dma_start(w2_sb[:], w2.rearrange("(p k) m -> p k m", k=BLOCKS))
-        nc.scalar.dma_start(b1_sb[:], b1.rearrange("(p m) o -> p (m o)", m=BLOCKS))
-        nc.scalar.dma_start(b2_sb[:], b2.rearrange("(p m) o -> p (m o)", m=BLOCKS))
 
         h = [held.tile([P, N], F32, name=f"h{b}") for b in range(BLOCKS)]
         h_bf = [held.tile([P, N], BF16, name=f"h_bf{b}") for b in range(BLOCKS)]

@@ -48,10 +48,12 @@ def tile_kanex_kernel(tc, tok_emb, pos_emb, w1, b1, w2, b2, offs, out):
         nc.sync.dma_start(pos[0][:], pos_blocks[:, 0, :])
         nc.sync.dma_start(w1_sb[:], w1.rearrange("(p k) m -> p k m", k=BLOCKS))
         nc.sync.dma_start(table[1][:], tok_blocks[:, 1, :])
-        nc.sync.dma_start(pos[1][:, : WIDTHS[0]], pos_blocks[:, 1, : WIDTHS[0]])
+        for piece in pieces[:2]:
+            nc.sync.dma_start(pos[1][:, piece], pos_blocks[:, 1, piece])
         nc.sync.dma_start(b1_sb[:], b1.rearrange("(p m) o -> p (m o)", m=BLOCKS))
         nc.sync.dma_start(b2_sb[:], b2.rearrange("(p m) o -> p (m o)", m=BLOCKS))
-        nc.sync.dma_start(pos[1][:, WIDTHS[0] :], pos_blocks[:, 1, WIDTHS[0] :])
+        rest = slice(pieces[2].start, N)
+        nc.sync.dma_start(pos[1][:, rest], pos_blocks[:, 1, rest])
         nc.sync.dma_start(w2_sb[:], w2.rearrange("(p k) m -> p k m", k=BLOCKS))
 
         h = [held.tile([P, N], F32, name=f"h{b}") for b in range(BLOCKS)]
@@ -99,7 +101,10 @@ def tile_kanex_kernel(tc, tok_emb, pos_emb, w1, b1, w2, b2, offs, out):
 
         for j in range(PIECES):
             lookup_add(1, j)
-            nc.vector.tensor_copy(h_bf[1][:, pieces[j]], h[1][:, pieces[j]])
+            if j < 2:
+                nc.scalar.copy(h_bf[1][:, pieces[j]], h[1][:, pieces[j]])
+            else:
+                nc.vector.tensor_copy(h_bf[1][:, pieces[j]], h[1][:, pieces[j]])
             layer1(1, j)
             for m in range(BLOCKS):
                 nc.scalar.activation(u_bf[m][:, pieces[j]], acc1[j][m][:], SILU, bias=b1_sb[:, m : m + 1])

@@ -10,7 +10,8 @@ C = 256
 BLOCKS = C // P
 WORDS = 2048
 N = 1024
-WIDTHS = (256, 256, 256, 256)
+STEP = 32
+WIDTHS = (256 - STEP, 256 + STEP, 256 + STEP, 256 - STEP)
 PIECES = len(WIDTHS)
 BANKS = 8
 PER_COLUMN = 16
@@ -46,10 +47,12 @@ def tile_kanex_kernel(tc, tok_emb, pos_emb, w1, b1, w2, b2, offs, out):
         nc.sync.dma_start(table[0][:], tok_blocks[:, 0, :])
         nc.sync.dma_start(offsets[:], offs)
         nc.sync.dma_start(pos[0][:], pos_blocks[:, 0, :])
-        nc.sync.dma_start(w1_sb[:], w1.rearrange("(p k) m -> p k m", k=BLOCKS))
+        w1_halves = w1.rearrange("(p k) m -> p k m", k=BLOCKS)
+        nc.sync.dma_start(w1_sb[:, 0, :], w1_halves[:, 0, :])
         nc.sync.dma_start(table[1][:], tok_blocks[:, 1, :])
         for piece in pieces[:2]:
             nc.sync.dma_start(pos[1][:, piece], pos_blocks[:, 1, piece])
+        nc.sync.dma_start(w1_sb[:, 1, :], w1_halves[:, 1, :])
         nc.sync.dma_start(b1_sb[:], b1.rearrange("(p m) o -> p (m o)", m=BLOCKS))
         nc.sync.dma_start(b2_sb[:], b2.rearrange("(p m) o -> p (m o)", m=BLOCKS))
         rest = slice(pieces[2].start, N)

@@ -11,7 +11,7 @@ BLOCKS = C // P
 WORDS = 2048
 N = 1024
 STEP = 32
-WIDTHS = (256 - STEP, 256 + STEP, 256 + STEP, 256 - STEP)
+WIDTHS = (256 - STEP, 256 + STEP, 256, 256)
 PIECES = len(WIDTHS)
 BANKS = 8
 PER_COLUMN = 16
@@ -80,12 +80,13 @@ def tile_kanex_kernel(tc, tok_emb, pos_emb, w1, b1, w2, b2, offs, out):
 
         def layer2(j):
             acc2 = [psum.tile([P, WIDTHS[j]], F32, name="acc") for m in range(BLOCKS)]
-            for k in range(BLOCKS):
-                for m in range(BLOCKS):
-                    nc.tensor.matmul(
-                        acc2[m][:], w2_sb[:, k, m::BLOCKS], u_bf[k][:, pieces[j]],
-                        start=(k == 0), stop=(k == BLOCKS - 1),
-                    )
+            u_first = [(k, m) for k in range(BLOCKS) for m in range(BLOCKS)]
+            p_first = [(k, m) for m in range(BLOCKS) for k in range(BLOCKS)]
+            for k, m in p_first if j > 0 else u_first:
+                nc.tensor.matmul(
+                    acc2[m][:], w2_sb[:, k, m::BLOCKS], u_bf[k][:, pieces[j]],
+                    start=(k == 0), stop=(k == BLOCKS - 1),
+                )
             nc.vector.tensor_scalar_add(p_sb[:, 0, pieces[j]], acc2[0][:], b2_sb[:, 0:1])
             if j < PIECES // 2:
                 nc.vector.tensor_scalar_add(p_sb[:, 1, pieces[j]], acc2[1][:], b2_sb[:, 1:2])

import concourse.mybir as mybir

F32, BF16, U16 = mybir.dt.float32, mybir.dt.bfloat16, mybir.dt.uint16
ADD = mybir.AluOpType.add
SILU = mybir.ActivationFunctionType.Silu
IDENTITY = mybir.ActivationFunctionType.Identity

P = 128
C = 256
BLOCKS = C // P
WORDS = 2048
N = 1024
STEP = 32
WIDTHS = (256 - STEP, 256 + STEP, 256, 256)
PIECES = len(WIDTHS)
BANKS = 8
PER_COLUMN = 16

FLOPS = 2 * 2 * C * C * N


def tile_kanex_kernel(tc, tok_emb, pos_emb, w1, b1, w2, b2, offs, out):
    nc = tc.nc
    tok_blocks = tok_emb.rearrange("(p b) s -> p b s", b=BLOCKS)
    pos_blocks = pos_emb.rearrange("(p b) n -> p b n", b=BLOCKS)
    h_out = out[:C, :].rearrange("(p b) n -> p b n", b=BLOCKS)
    p_out = out[C:, :].rearrange("(p b) n -> p b n", b=BLOCKS)
    pieces = [slice(sum(WIDTHS[:j]), sum(WIDTHS[: j + 1])) for j in range(PIECES)]
    with (
        tc.tile_pool(name="held", bufs=1) as held,
        tc.psum_pool(name="psum", bufs=BANKS) as psum,
    ):
        offsets = held.tile([P, N // PER_COLUMN], U16, name="offsets")

        table = [held.tile([P, WORDS], F32, name=f"table{b}") for b in range(BLOCKS)]
        pos = [held.tile([P, N], F32, name=f"pos{b}") for b in range(BLOCKS)]
        w1_sb = held.tile([P, BLOCKS, C], BF16, name="w1_sb")
        w2_sb = held.tile([P, BLOCKS, C], BF16, name="w2_sb")
        b1_sb = held.tile([P, BLOCKS], F32, name="b1_sb")
        b2_sb = held.tile([P, BLOCKS], F32, name="b2_sb")

        zeros = held.tile([P, 1], F32, name="zeros")
        unread = held.tile([P, 1], F32, name="unread")
        nc.vector.memset(zeros[:], 0.0)
        nc.scalar.activation(unread[:], zeros[:], SILU)

        nc.sync.dma_start(table[0][:], tok_blocks[:, 0, :])
        nc.sync.dma_start(offsets[:], offs)
        nc.sync.dma_start(pos[0][:], pos_blocks[:, 0, :])
        w1_halves = w1.rearrange("(p k) m -> p k m", k=BLOCKS)
        nc.sync.dma_start(w1_sb[:, 0, :], w1_halves[:, 0, :])
        nc.sync.dma_start(table[1][:], tok_blocks[:, 1, :])
        for piece in pieces[:2]:
            nc.sync.dma_start(pos[1][:, piece], pos_blocks[:, 1, piece])
        nc.sync.dma_start(w1_sb[:, 1, :], w1_halves[:, 1, :])
        nc.sync.dma_start(b1_sb[:], b1.rearrange("(p m) o -> p (m o)", m=BLOCKS))
        nc.sync.dma_start(b2_sb[:], b2.rearrange("(p m) o -> p (m o)", m=BLOCKS))
        rest = slice(pieces[2].start, N)
        nc.sync.dma_start(pos[1][:, rest], pos_blocks[:, 1, rest])
        nc.sync.dma_start(w2_sb[:], w2.rearrange("(p k) m -> p k m", k=BLOCKS))

        h = [held.tile([P, N], F32, name=f"h{b}") for b in range(BLOCKS)]
        h_bf = [held.tile([P, N], BF16, name=f"h_bf{b}") for b in range(BLOCKS)]
        u_bf = [held.tile([P, N], BF16, name=f"u_bf{m}") for m in range(BLOCKS)]
        p_sb = held.tile([P, BLOCKS, N], F32, name="p_sb")

        def lookup_add(b, j):
            some = offsets[:, pieces[j].start // PER_COLUMN : pieces[j].stop // PER_COLUMN]
            nc.vector.tensor_tensor(h[b][:, pieces[j]], table[b][:].indirect(some), pos[b][:, pieces[j]], ADD)
            if j % 2 == 1:
                pair = slice(pieces[j - 1].start, pieces[j].stop)
                nc.sync.dma_start(h_out[:, b, pair], h[b][:, pair])

        def layer1(k, j):
            for m in range(BLOCKS):
                nc.tensor.matmul(
                    acc1[j][m][:], w1_sb[:, k, m::BLOCKS], h_bf[k][:, pieces[j]],
                    start=(k == 0), stop=(k == BLOCKS - 1),
                )

        def layer2(j):
            acc2 = [psum.tile([P, WIDTHS[j]], F32, name="acc") for m in range(BLOCKS)]
            u_first = [(k, m) for k in range(BLOCKS) for m in range(BLOCKS)]
            p_first = [(k, m) for m in range(BLOCKS) for k in range(BLOCKS)]
            for k, m in p_first if j > 0 else u_first:
                nc.tensor.matmul(
                    acc2[m][:], w2_sb[:, k, m::BLOCKS], u_bf[k][:, pieces[j]],
                    start=(k == 0), stop=(k == BLOCKS - 1),
                )
            nc.vector.tensor_scalar_add(p_sb[:, 0, pieces[j]], acc2[0][:], b2_sb[:, 0:1])
            if j < PIECES // 2:
                nc.vector.tensor_scalar_add(p_sb[:, 1, pieces[j]], acc2[1][:], b2_sb[:, 1:2])
            else:
                nc.scalar.activation(p_sb[:, 1, pieces[j]], acc2[1][:], IDENTITY, bias=b2_sb[:, 1:2])

        def store_p(j):
            for m in range(BLOCKS):
                nc.sync.dma_start(p_out[:, m, pieces[j]], p_sb[:, m, pieces[j]])

        acc1 = [[psum.tile([P, WIDTHS[j]], F32, name="acc") for m in range(BLOCKS)] for j in range(PIECES)]
        for j in range(PIECES):
            lookup_add(0, j)
            nc.scalar.copy(h_bf[0][:, pieces[j]], h[0][:, pieces[j]])
            layer1(0, j)

        for j in range(PIECES):
            lookup_add(1, j)
            if j < 2:
                nc.scalar.copy(h_bf[1][:, pieces[j]], h[1][:, pieces[j]])
            else:
                nc.vector.tensor_copy(h_bf[1][:, pieces[j]], h[1][:, pieces[j]])
            layer1(1, j)
            for m in range(BLOCKS):
                nc.scalar.activation(u_bf[m][:, pieces[j]], acc1[j][m][:], SILU, bias=b1_sb[:, m : m + 1])
            if j == 1:
                layer2(0)
        store_p(0)
        for j in range(1, PIECES):
            layer2(j)
            store_p(j)
